import numpy as np
import ml_dtypes


def mxq(x, axis, fmt="e4m3"):
    dtype, down = {"e4m3": (ml_dtypes.float8_e4m3fn, 7), "e5m2": (ml_dtypes.float8_e5m2, 14)}[fmt]
    v = np.moveaxis(np.asarray(x, np.float32).astype(ml_dtypes.bfloat16).astype(np.float64), axis, -1)
    blocks = v.reshape(v.shape[:-1] + (-1, 32))
    amax = np.abs(blocks).max(-1, keepdims=True)
    byte = np.maximum(np.where(amax > 0, np.frexp(amax)[1] - 1 + 127, 0) - down, 1)
    scale = np.exp2(byte - 127.0)
    codes = (blocks / scale).astype(np.float32).astype(dtype).astype(np.float64)
    return np.moveaxis((codes * scale).reshape(v.shape), -1, axis)


WIDE = False


def mx_kscale(k):
    if not WIDE:
        return np.ones(k)
    levels = np.array([10, -10, 5, -5, 0])
    if k % 512:
        return np.exp2(np.random.permutation(np.resize(levels, k // 32))).repeat(32)
    a = np.empty((k // 512, 16))
    for p in range(k // 512):
        a[p, :8] = np.random.permutation(np.resize(levels, 8))
        for g in range(8):
            far = levels[np.abs(levels - a[p, g]) >= 10]
            a[p, g + 8] = far[np.random.randint(len(far))]
    return np.exp2(a.ravel()).repeat(32)


BF16 = ml_dtypes.bfloat16


def bf(x):
    return np.asarray(x, np.float32).astype(BF16)


def f64(x):
    return np.asarray(x).astype(np.float64)


B, CL, CH, CK, CV, CO, H, W = 2, 1024, 2048, 256, 512, 1024, 24, 24
N = H * W
CF = CO + CH
EPS = 1e-5


def setup_inputs():
    s = mx_kscale(CV)
    t = mx_kscale(CF)
    tc, th = t[:CO], t[CO:]
    return {"context": bf(np.random.standard_normal((B, CV, H, W)) * 0.4 * s[None, :, None, None]),
            "high_feats": bf(np.random.standard_normal((B, CH, H, W)) * th[None, :, None, None]),
            "ww": bf(np.random.standard_normal((CO, CV)) * 2.0 / np.sqrt(CV) / s[None, :] * tc[:, None]),
            "bw": bf(np.random.standard_normal(CO) * 0.3 * tc),
            "wf": bf(np.random.standard_normal((CO, CF)) / np.sqrt(CF) / t[None, :]),
            "bfuse": bf(np.random.standard_normal(CO) * 0.3),
            "gf": bf(np.random.uniform(0.5, 1.5, CO)),
            "bef": bf(np.random.standard_normal(CO) * 0.3),
            "mf": bf(np.random.standard_normal(CO) * 0.3),
            "vf": bf(np.random.uniform(0.5, 1.5, CO))}


def reference(context, high_feats, ww, bw, wf, bfuse, gf, bef, mf, vf):
    ctx = f64(context).reshape(B, CV, N)
    hi = f64(high_feats).reshape(B, CH, N)
    c = (mxq(f64(ww), 1, "e4m3") @ mxq(ctx, 1, "e4m3")) + f64(bw)[None, :, None]
    fused = np.concatenate([c, hi], axis=1)
    y = (mxq(f64(wf), 1, "e4m3") @ mxq(fused, 1, "e4m3")) + f64(bfuse)[None, :, None]
    sc = f64(gf) / np.sqrt(f64(vf) + EPS)
    out = (y - f64(mf)[None, :, None]) * sc[None, :, None] + f64(bef)[None, :, None]
    return out.reshape(B, CO, H, W)

@@ -1,0 +1,302 @@
+from contextlib import ExitStack
+
+import concourse.mybir as mybir
+from concourse.masks import make_identity
+
+F32 = mybir.dt.float32
+BF16 = mybir.dt.bfloat16
+U32 = mybir.dt.uint32
+U8 = mybir.dt.uint8
+FP8X4 = mybir.dt.float8_e4m3fn_x4
+ACT = mybir.ActivationFunctionType
+
+P = 128
+PACK = 4
+K_PASS = P * PACK
+WORDS_PASS = K_PASS // 2
+
+IMAGES = 2
+PIXELS = 24 * 24
+COLS = IMAGES * PIXELS
+C_CTX = 512
+C_MID = 1024
+C_HIGH = 2048
+C_FUSED = C_MID + C_HIGH
+C_OUT = 1024
+EPS = 1e-5
+
+MID_TILES = C_MID // P
+MID_PASSES = C_MID // K_PASS
+HIGH_PASSES = C_HIGH // K_PASS
+FUSED_PASSES = MID_PASSES + HIGH_PASSES
+OUT_TILES = C_OUT // P
+HALF = OUT_TILES // 2
+
+CHUNK = 512
+CHUNKS = ((0, 512), (512, 512), (1024, 128))
+WF_AHEAD = 2
+
+STEPS = 4 * HALF
+FIRST_BLOCK_STEP = STEPS // 2
+BLOCKS = 1 + HIGH_PASSES + MID_PASSES
+FIRST_C_STEP = FIRST_BLOCK_STEP + 1
+C_TILES_A_STEP = 2
+
+FLOPS = 2 * COLS * (C_MID * C_CTX + C_OUT * C_FUSED)
+
+
+def image_pieces(col0, width):
+    pieces = []
+    for image in range(IMAGES):
+        lo = max(col0, image * PIXELS)
+        hi = min(col0 + width, (image + 1) * PIXELS)
+        if lo < hi:
+            pieces.append((image, lo - image * PIXELS, hi - lo, lo - col0))
+    return pieces
+
+
+def tile_afnb_pb_kernel(tc, context, high_feats, ww, bw, wf, bfuse, gf, bef, mf, vf, out):
+    nc = tc.nc
+    with ExitStack() as ctx:
+        keep = ctx.enter_context(tc.tile_pool(name="keep", bufs=1))
+        stage = ctx.enter_context(tc.tile_pool(name="stage", bufs=4))
+        short_banks = ctx.enter_context(tc.psum_pool(name="short_banks", bufs=4))
+        sum_banks = ctx.enter_context(tc.psum_pool(name="sum_banks", bufs=HALF))
+
+        identity = keep.tile([P, P], F32)
+        make_identity(nc, identity[:])
+
+        bw_bf = keep.tile([P, MID_TILES], BF16)
+        nc.scalar.dma_start(
+            out=bw_bf[:].rearrange("p (g t) -> p g t", t=PACK),
+            in_=bw.rearrange("(g p t) -> p g t", p=P, t=PACK),
+        )
+        per_channel = {}
+        for name, vector in (("vf", vf), ("gf", gf), ("bfuse", bfuse), ("mf", mf), ("bef", bef)):
+            per_channel[name] = keep.tile([P, OUT_TILES], BF16, name=name + "_bf")
+            nc.scalar.dma_start(out=per_channel[name][:], in_=vector.rearrange("(p m) -> p m", m=OUT_TILES))
+
+        def load_activations(rows, name):
+            raw = keep.tile([P, PACK, PIXELS], BF16, name=name)
+            nc.sync.dma_start(out=raw[:], in_=rows.rearrange("(p t) h w -> p t (h w)", t=PACK))
+            return raw
+
+        ctx_raw = [None] * IMAGES
+        high_raw = [[None] * HIGH_PASSES for image in range(IMAGES)]
+        wf_raw = [None] * OUT_TILES
+
+        def load_context(image):
+            ctx_raw[image] = load_activations(context[image], "ctx_raw%d" % image)
+
+        def load_high(image, h):
+            high_raw[image][h] = load_activations(
+                high_feats[image, h * K_PASS : (h + 1) * K_PASS], "high_raw%d_%d" % (image, h)
+            )
+
+        def load_wf(m):
+            wf_raw[m] = keep.tile([P, C_FUSED], BF16, name="wf_raw%d" % m)
+            nc.sync.dma_start(out=wf_raw[m][:], in_=wf.rearrange("(p m) k -> p m k", m=OUT_TILES)[:, m, :])
+
+        load_context(0)
+        load_high(0, 0)
+        ww_raw = keep.tile([P, MID_TILES * C_CTX], BF16)
+        nc.sync.dma_start(
+            out=ww_raw[:].rearrange("p (g t k) -> p g t k", t=PACK, k=C_CTX),
+            in_=ww.rearrange("(g p t) k -> p g t k", p=P, t=PACK),
+        )
+        load_high(0, 1)
+        load_high(0, 2)
+        load_wf(0)
+        load_high(0, 3)
+        for m in range(1, OUT_TILES):
+            load_wf(m)
+        load_context(1)
+        for h in range(HIGH_PASSES):
+            load_high(1, h)
+
+        ww_codes = keep.tile([P, MID_TILES * P], U32, align_bytes=64)
+        ww_scales = keep.tile([P, MID_TILES * P], U8, align_bytes=64)
+        wf_codes = keep.tile([P, OUT_TILES * FUSED_PASSES * P], U32, align_bytes=64)
+        wf_scales = keep.tile([P, OUT_TILES * FUSED_PASSES * P], U8, align_bytes=64)
+        ctx_codes = keep.tile([P, COLS], U32, align_bytes=64)
+        ctx_scales = keep.tile([P, COLS], U8, align_bytes=64)
+        fused_codes = keep.tile([P, FUSED_PASSES, COLS], U32, align_bytes=64)
+        fused_scales = keep.tile([P, FUSED_PASSES, COLS], U8, align_bytes=64)
+
+        def transpose_weights(raw, pairs):
+            words = raw[:].bitcast(F32)
+            grouped_pairs = []
+            for pair in range(pairs):
+                flipped = short_banks.tile([P, 4, P], F32, name="short")
+                for q in range(4):
+                    a, u = divmod(q, 2)
+                    first = (2 * pair + a) * WORDS_PASS
+                    nc.tensor.transpose(
+                        flipped[:, q, :], words[:, first + u : first + WORDS_PASS : 2], identity[:]
+                    )
+                grouped = stage.tile([P, 2 * P * PACK], BF16, name="w_grouped", bufs=6, align_bytes=64)
+                nc.scalar.copy(
+                    out=grouped[:].bitcast(F32).rearrange("p (a r u) -> p a r u", a=2, u=2),
+                    in_=flipped[:].rearrange("p (a u) r -> p a r u", u=2),
+                )
+                grouped_pairs.append(grouped)
+            return grouped_pairs
+
+        def quantise_weights(grouped_pairs, codes, scales, first_operand):
+            for pair, grouped in enumerate(grouped_pairs):
+                cols = slice((first_operand + 2 * pair) * P, (first_operand + 2 * pair + 2) * P)
+                nc.vector.quantize_mx(out=codes[:, cols].bitcast(FP8X4), scales=scales[:, cols], in_=grouped[:])
+
+        wf_grouped = [None] * OUT_TILES
+
+        def transpose_wf(m):
+            wf_grouped[m] = transpose_weights(wf_raw[m], FUSED_PASSES // 2)
+
+        def quantise_wf(m):
+            quantise_weights(wf_grouped[m], wf_codes, wf_scales, m * FUSED_PASSES)
+
+        def regroup(sources):
+            grouped = stage.tile([P, CHUNK, PACK], BF16, name="a_grouped", align_bytes=64)
+            for rows, first, number, offset in sources:
+                nc.vector.tensor_copy(
+                    out=grouped[:, offset : offset + number, :].rearrange("p (c i) t -> p c t i", i=4),
+                    in_=rows[:, :, first : first + number].rearrange("p t (c i) -> p c t i", i=4),
+                )
+            return grouped
+
+        def quantise(grouped, width, codes, scales):
+            nc.vector.quantize_mx(
+                out=codes.bitcast(FP8X4),
+                scales=scales,
+                in_=grouped[:, :width, :].rearrange("p c t -> p (c t)"),
+            )
+
+        c_rows = [None] * MID_PASSES
+
+        def regroup_block(block, col0, width):
+            pieces = image_pieces(col0, width)
+            if block == 0:
+                return regroup([(ctx_raw[image], first, number, offset) for image, first, number, offset in pieces])
+            if block <= HIGH_PASSES:
+                return regroup(
+                    [(high_raw[image][block - 1], first, number, offset) for image, first, number, offset in pieces]
+                )
+            return regroup([(c_rows[block - 1 - HIGH_PASSES], 0, width, 0)])
+
+        def quantise_block(block, grouped, col0, width):
+            cols = slice(col0, col0 + width)
+            if block == 0:
+                quantise(grouped, width, ctx_codes[:, cols], ctx_scales[:, cols])
+            else:
+                g = MID_PASSES + block - 1 if block <= HIGH_PASSES else block - 1 - HIGH_PASSES
+                quantise(grouped, width, fused_codes[:, g, cols], fused_scales[:, g, cols])
+
+        def c_tile(j, col0, width):
+            cols = slice(col0, col0 + width)
+            g, t = divmod(j, PACK)
+            if t == 0:
+                c_rows[g] = stage.tile([P, PACK, CHUNK], BF16, name="c_rows", bufs=MID_PASSES)
+            c_sum = short_banks.tile([P, CHUNK], F32, name="short")
+            nc.tensor.matmul_mx(
+                out=c_sum[:, :width],
+                lhsT=ww_codes[:, j * P : (j + 1) * P].bitcast(FP8X4),
+                lhsT_scale=ww_scales[:, j * P : (j + 1) * P],
+                rhs=ctx_codes[:, cols].bitcast(FP8X4),
+                rhs_scale=ctx_scales[:, cols],
+                start=True,
+                stop=True,
+            )
+            nc.scalar.activation(
+                out=c_rows[g][:, t, :width], in_=c_sum[:, :width], func=ACT.Identity,
+                bias=bw_f32[:, j : j + 1], scale=1.0,
+            )
+
+        def y_passes(y_sum, m, passes, col0, width):
+            cols = slice(col0, col0 + width)
+            for g in passes:
+                w_cols = slice((m * FUSED_PASSES + g) * P, (m * FUSED_PASSES + g + 1) * P)
+                nc.tensor.matmul_mx(
+                    out=y_sum[:, :width],
+                    lhsT=wf_codes[:, w_cols].bitcast(FP8X4),
+                    lhsT_scale=wf_scales[:, w_cols],
+                    rhs=fused_codes[:, g, cols].bitcast(FP8X4),
+                    rhs_scale=fused_scales[:, g, cols],
+                    start=(g == MID_PASSES),
+                    stop=(g == MID_PASSES - 1),
+                )
+
+        def finish_tile(y_sum, m, col0, width):
+            result = stage.tile(
+                [P, width], F32, name="result%d" % width, bufs=(HALF if width == CHUNK else OUT_TILES)
+            )
+            nc.scalar.activation(
+                out=result[:, :width], in_=y_sum[:, :width], func=ACT.Identity,
+                bias=shift[:, m : m + 1], scale=gain[:, m : m + 1],
+            )
+            for image, first, number, offset in image_pieces(col0, width):
+                nc.sync.dma_start(
+                    out=out[image].rearrange("(p m) h w -> p m (h w)", m=OUT_TILES)[:, m, first : first + number],
+                    in_=result[:, offset : offset + number],
+                )
+
+        first_chunk = CHUNKS[0]
+        bw_f32 = keep.tile([P, MID_TILES], F32)
+        gain = keep.tile([P, OUT_TILES], F32)
+        shift = keep.tile([P, OUT_TILES], F32)
+        nc.vector.tensor_scalar_add(out=gain[:], in0=per_channel["vf"][:], scalar1=EPS)
+        nc.scalar.sqrt(out=gain[:], in_=gain[:])
+        nc.vector.tensor_copy(out=bw_f32[:], in_=bw_bf[:])
+
+        for block in (0, 1):
+            quantise_block(block, regroup_block(block, *first_chunk), *first_chunk)
+        nc.vector.reciprocal(out=gain[:], in_=gain[:])
+        nc.vector.tensor_mul(out=gain[:], in0=gain[:], in1=per_channel["gf"][:])
+        nc.vector.tensor_sub(out=shift[:], in0=per_channel["bfuse"][:], in1=per_channel["mf"][:])
+        nc.vector.tensor_mul(out=shift[:], in0=shift[:], in1=gain[:])
+        nc.vector.tensor_add(out=shift[:], in0=shift[:], in1=per_channel["bef"][:])
+
+        quantise_weights(transpose_weights(ww_raw, MID_TILES // 2), ww_codes, ww_scales, 0)
+        for j in range(PACK):
+            c_tile(j, *first_chunk)
+        grouped_2 = regroup_block(2, *first_chunk)
+        grouped_3 = regroup_block(3, *first_chunk)
+        quantise_block(2, grouped_2, *first_chunk)
+        quantise_block(3, grouped_3, *first_chunk)
+        transpose_wf(0)
+        for j in range(PACK, MID_TILES):
+            c_tile(j, *first_chunk)
+        grouped_4 = regroup_block(4, *first_chunk)
+        quantise_wf(0)
+        quantise_block(4, grouped_4, *first_chunk)
+        transpose_wf(1)
+        grouped_5 = regroup_block(5, *first_chunk)
+        quantise_wf(1)
+        quantise_block(5, grouped_5, *first_chunk)
+        quantise_block(6, regroup_block(6, *first_chunk), *first_chunk)
+
+        def prepare_next(index, step):
+            if index + 1 == len(CHUNKS):
+                return
+            following = CHUNKS[index + 1]
+            for j in range(C_TILES_A_STEP * (step - FIRST_C_STEP), C_TILES_A_STEP * (step - FIRST_C_STEP + 1)):
+                if 0 <= j < MID_TILES:
+                    c_tile(j, *following)
+            block = step - FIRST_BLOCK_STEP
+            if 0 <= block < BLOCKS:
+                quantise_block(block, regroup_block(block, *following), *following)
+
+        for index, (col0, width) in enumerate(CHUNKS):
+            for half in range(2):
+                tiles = range(half * HALF, (half + 1) * HALF)
+                y_sums = {}
+                for m in tiles:
+                    prepare_next(index, 2 * half * HALF + m % HALF)
+                    y_sums[m] = sum_banks.tile([P, CHUNK], F32, name="y_sum")
+                    y_passes(y_sums[m], m, range(MID_PASSES, FUSED_PASSES), col0, width)
+                    if index == 0 and m + WF_AHEAD < OUT_TILES:
+                        transpose_wf(m + WF_AHEAD)
+                        quantise_wf(m + WF_AHEAD)
+                for m in tiles:
+                    prepare_next(index, (2 * half + 1) * HALF + m % HALF)
+                    y_passes(y_sums[m], m, range(MID_PASSES), col0, width)
+                    finish_tile(y_sums[m], m, col0, width)

@@ -58,6 +58,7 @@ def image_pieces(col0, width):
 def tile_afnb_pb_kernel(tc, context, high_feats, ww, bw, wf, bfuse, gf, bef, mf, vf, out):
     nc = tc.nc
     with ExitStack() as ctx:
+        ctx.enter_context(tc.manual_schedule())
         keep = ctx.enter_context(tc.tile_pool(name="keep", bufs=1))
         stage = ctx.enter_context(tc.tile_pool(name="stage", bufs=4))
         short_banks = ctx.enter_context(tc.psum_pool(name="short_banks", bufs=4))
@@ -65,16 +66,6 @@ def tile_afnb_pb_kernel(tc, context, high_feats, ww, bw, wf, bfuse, gf, bef, mf,
 
         identity = keep.tile([P, P], F32)
         make_identity(nc, identity[:])
-
-        bw_bf = keep.tile([P, MID_TILES], BF16)
-        nc.scalar.dma_start(
-            out=bw_bf[:].rearrange("p (g t) -> p g t", t=PACK),
-            in_=bw.rearrange("(g p t) -> p g t", p=P, t=PACK),
-        )
-        per_channel = {}
-        for name, vector in (("vf", vf), ("gf", gf), ("bfuse", bfuse), ("mf", mf), ("bef", bef)):
-            per_channel[name] = keep.tile([P, OUT_TILES], BF16, name=name + "_bf")
-            nc.scalar.dma_start(out=per_channel[name][:], in_=vector.rearrange("(p m) -> p m", m=OUT_TILES))
 
         def load_activations(rows, name):
             raw = keep.tile([P, PACK, PIXELS], BF16, name=name)
@@ -97,18 +88,40 @@ def tile_afnb_pb_kernel(tc, context, high_feats, ww, bw, wf, bfuse, gf, bef, mf,
             wf_raw[m] = keep.tile([P, C_FUSED], BF16, name="wf_raw%d" % m)
             nc.sync.dma_start(out=wf_raw[m][:], in_=wf.rearrange("(p m) k -> p m k", m=OUT_TILES)[:, m, :])
 
+        ww_raw = [None] * MID_PASSES
+
+        def load_ww(g):
+            ww_raw[g] = keep.tile([P, PACK * C_CTX], BF16, name="ww_raw%d" % g)
+            nc.sync.dma_start(
+                out=ww_raw[g][:],
+                in_=ww[g * K_PASS : (g + 1) * K_PASS, :].rearrange("(p t) k -> p (t k)", t=PACK),
+            )
+
+        bw_bf = keep.tile([P, MID_TILES], BF16)
+        per_channel = {}
+
+        def load_bw():
+            nc.sync.dma_start(
+                out=bw_bf[:].rearrange("p (g t) -> p g t", t=PACK),
+                in_=bw.rearrange("(g p t) -> p g t", p=P, t=PACK),
+            )
+
+        def load_norm():
+            for name, vector in (("vf", vf), ("gf", gf), ("bfuse", bfuse), ("mf", mf), ("bef", bef)):
+                per_channel[name] = keep.tile([P, OUT_TILES], BF16, name=name + "_bf")
+                nc.sync.dma_start(out=per_channel[name][:], in_=vector.rearrange("(p m) -> p m", m=OUT_TILES))
+
+        load_ww(0)
         load_context(0)
-        load_high(0, 0)
-        ww_raw = keep.tile([P, MID_TILES * C_CTX], BF16)
-        nc.sync.dma_start(
-            out=ww_raw[:].rearrange("p (g t k) -> p g t k", t=PACK, k=C_CTX),
-            in_=ww.rearrange("(g p t) k -> p g t k", p=P, t=PACK),
-        )
-        load_high(0, 1)
-        load_high(0, 2)
+        load_ww(1)
         load_wf(0)
-        load_high(0, 3)
-        for m in range(1, OUT_TILES):
+        load_bw()
+        for i in range(HIGH_PASSES):
+            load_high(0, i)
+            load_wf(i + 1)
+            if i == 0:
+                load_norm()
+        for m in range(HIGH_PASSES + 1, OUT_TILES):
             load_wf(m)
         load_context(1)
         for h in range(HIGH_PASSES):
@@ -191,12 +204,13 @@ def tile_afnb_pb_kernel(tc, context, high_feats, ww, bw, wf, bfuse, gf, bef, mf,
                 g = MID_PASSES + block - 1 if block <= HIGH_PASSES else block - 1 - HIGH_PASSES
                 quantise(grouped, width, fused_codes[:, g, cols], fused_scales[:, g, cols])
 
-        def c_tile(j, col0, width):
+        def c_tile(j, col0, width, banks):
             cols = slice(col0, col0 + width)
             g, t = divmod(j, PACK)
             if t == 0:
                 c_rows[g] = stage.tile([P, PACK, CHUNK], BF16, name="c_rows", bufs=MID_PASSES)
-            c_sum = short_banks.tile([P, CHUNK], F32, name="short")
+            pool, name = banks
+            c_sum = pool.tile([P, CHUNK], F32, name=name)
             nc.tensor.matmul_mx(
                 out=c_sum[:, :width],
                 lhsT=ww_codes[:, j * P : (j + 1) * P].bitcast(FP8X4),
@@ -208,7 +222,7 @@ def tile_afnb_pb_kernel(tc, context, high_feats, ww, bw, wf, bfuse, gf, bef, mf,
             )
             nc.scalar.activation(
                 out=c_rows[g][:, t, :width], in_=c_sum[:, :width], func=ACT.Identity,
-                bias=bw_f32[:, j : j + 1], scale=1.0,
+                bias=bw_bf[:, j : j + 1], scale=1.0,
             )
 
         def y_passes(y_sum, m, passes, col0, width):
@@ -240,39 +254,60 @@ def tile_afnb_pb_kernel(tc, context, high_feats, ww, bw, wf, bfuse, gf, bef, mf,
                 )
 
         first_chunk = CHUNKS[0]
-        bw_f32 = keep.tile([P, MID_TILES], F32)
         gain = keep.tile([P, OUT_TILES], F32)
         shift = keep.tile([P, OUT_TILES], F32)
-        nc.vector.tensor_scalar_add(out=gain[:], in0=per_channel["vf"][:], scalar1=EPS)
-        nc.scalar.sqrt(out=gain[:], in_=gain[:])
-        nc.vector.tensor_copy(out=bw_f32[:], in_=bw_bf[:])
+        short = (short_banks, "short")
+        sums = (sum_banks, "y_sum")
 
-        for block in (0, 1):
-            quantise_block(block, regroup_block(block, *first_chunk), *first_chunk)
-        nc.vector.reciprocal(out=gain[:], in_=gain[:])
-        nc.vector.tensor_mul(out=gain[:], in0=gain[:], in1=per_channel["gf"][:])
-        nc.vector.tensor_sub(out=shift[:], in0=per_channel["bfuse"][:], in1=per_channel["mf"][:])
-        nc.vector.tensor_mul(out=shift[:], in0=shift[:], in1=gain[:])
-        nc.vector.tensor_add(out=shift[:], in0=shift[:], in1=per_channel["bef"][:])
+        one = keep.tile([P, 1], F32)
+        nc.vector.memset(one[:], 1.0)
+        nc.scalar.sqrt(out=one[:], in_=one[:])
 
-        quantise_weights(transpose_weights(ww_raw, MID_TILES // 2), ww_codes, ww_scales, 0)
+        ww_grouped = [transpose_weights(ww_raw[g], PACK // 2) for g in range(MID_PASSES)]
+        grouped_ctx = regroup_block(0, *first_chunk)
+        quantise_weights(ww_grouped[0], ww_codes, ww_scales, 0)
+        quantise_block(0, grouped_ctx, *first_chunk)
+        quantise_weights(ww_grouped[1], ww_codes, ww_scales, PACK)
         for j in range(PACK):
-            c_tile(j, *first_chunk)
-        grouped_2 = regroup_block(2, *first_chunk)
-        grouped_3 = regroup_block(3, *first_chunk)
-        quantise_block(2, grouped_2, *first_chunk)
-        quantise_block(3, grouped_3, *first_chunk)
+            c_tile(j, *first_chunk, sums)
         transpose_wf(0)
-        for j in range(PACK, MID_TILES):
-            c_tile(j, *first_chunk)
-        grouped_4 = regroup_block(4, *first_chunk)
-        quantise_wf(0)
-        quantise_block(4, grouped_4, *first_chunk)
         transpose_wf(1)
-        grouped_5 = regroup_block(5, *first_chunk)
+        for j in range(PACK, MID_TILES):
+            c_tile(j, *first_chunk, sums)
+        transpose_wf(2)
+
+        y_sums = {}
+        grouped = [regroup_block(1, *first_chunk)]
+        quantise_wf(0)
+        quantise_block(1, grouped[0], *first_chunk)
+        grouped.append(regroup_block(2, *first_chunk))
         quantise_wf(1)
-        quantise_block(5, grouped_5, *first_chunk)
-        quantise_block(6, regroup_block(6, *first_chunk), *first_chunk)
+        for i in range(HALF):
+            quantise_block(2 + i, grouped[1 + i], *first_chunk)
+            grouped.append(regroup_block(3 + i, *first_chunk))
+            if i == 0:
+                nc.vector.tensor_scalar_add(out=gain[:], in0=per_channel["vf"][:], scalar1=EPS)
+                nc.scalar.sqrt(out=gain[:], in_=gain[:])
+                nc.vector.tensor_sub(out=shift[:], in0=per_channel["bfuse"][:], in1=per_channel["mf"][:])
+            elif i == 1:
+                nc.vector.reciprocal(out=gain[:], in_=gain[:])
+            elif i == 2:
+                nc.vector.tensor_mul(out=gain[:], in0=gain[:], in1=per_channel["gf"][:])
+            else:
+                nc.vector.tensor_mul(out=shift[:], in0=shift[:], in1=gain[:])
+            quantise_wf(i + 2)
+            for m in range(len(y_sums), min(i + 2, HALF)):
+                y_sums[m] = sum_banks.tile([P, CHUNK], F32, name="y_sum")
+                y_passes(y_sums[m], m, range(MID_PASSES, MID_PASSES + i), *first_chunk)
+            for m in y_sums:
+                y_passes(y_sums[m], m, (MID_PASSES + i,), *first_chunk)
+            if i + 3 < 6:
+                transpose_wf(i + 3)
+        quantise_block(6, grouped[5], *first_chunk)
+        nc.vector.tensor_add(out=shift[:], in0=shift[:], in1=per_channel["bef"][:])
+        for m in range(HALF):
+            y_passes(y_sums[m], m, range(MID_PASSES), *first_chunk)
+            finish_tile(y_sums[m], m, *first_chunk)
 
         def prepare_next(index, step):
             if index + 1 == len(CHUNKS):
@@ -280,13 +315,13 @@ def tile_afnb_pb_kernel(tc, context, high_feats, ww, bw, wf, bfuse, gf, bef, mf,
             following = CHUNKS[index + 1]
             for j in range(C_TILES_A_STEP * (step - FIRST_C_STEP), C_TILES_A_STEP * (step - FIRST_C_STEP + 1)):
                 if 0 <= j < MID_TILES:
-                    c_tile(j, *following)
+                    c_tile(j, *following, short)
             block = step - FIRST_BLOCK_STEP
             if 0 <= block < BLOCKS:
                 quantise_block(block, regroup_block(block, *following), *following)
 
         for index, (col0, width) in enumerate(CHUNKS):
-            for half in range(2):
+            for half in range(1 if index == 0 else 0, 2):
                 tiles = range(half * HALF, (half + 1) * HALF)
                 y_sums = {}
                 for m in tiles:

@@ -37,9 +37,9 @@ CHUNKS = ((0, 512), (512, 512), (1024, 128))
 WF_AHEAD = 2
 
 STEPS = 4 * HALF
-FIRST_BLOCK_STEP = STEPS // 2
+FIRST_BLOCK_STEP = STEPS // 2 - 1
 BLOCKS = 1 + HIGH_PASSES + MID_PASSES
-FIRST_C_STEP = FIRST_BLOCK_STEP + 1
+FIRST_C_STEP = FIRST_BLOCK_STEP + 3
 C_TILES_A_STEP = 2
 
 FLOPS = 2 * COLS * (C_MID * C_CTX + C_OUT * C_FUSED)
@@ -101,7 +101,7 @@ def tile_afnb_pb_kernel(tc, context, high_feats, ww, bw, wf, bfuse, gf, bef, mf,
         per_channel = {}
 
         def load_bw():
-            nc.sync.dma_start(
+            nc.scalar.dma_start(
                 out=bw_bf[:].rearrange("p (g t) -> p g t", t=PACK),
                 in_=bw.rearrange("(g p t) -> p g t", p=P, t=PACK),
             )
@@ -111,18 +111,18 @@ def tile_afnb_pb_kernel(tc, context, high_feats, ww, bw, wf, bfuse, gf, bef, mf,
                 per_channel[name] = keep.tile([P, OUT_TILES], BF16, name=name + "_bf")
                 nc.sync.dma_start(out=per_channel[name][:], in_=vector.rearrange("(p m) -> p m", m=OUT_TILES))
 
+        load_bw()
         load_ww(0)
         load_context(0)
         load_ww(1)
         load_wf(0)
-        load_bw()
         for i in range(HIGH_PASSES):
             load_high(0, i)
             load_wf(i + 1)
-            if i == 0:
-                load_norm()
         for m in range(HIGH_PASSES + 1, OUT_TILES):
             load_wf(m)
+            if m == HIGH_PASSES + 1:
+                load_norm()
         load_context(1)
         for h in range(HIGH_PASSES):
             load_high(1, h)
@@ -136,7 +136,7 @@ def tile_afnb_pb_kernel(tc, context, high_feats, ww, bw, wf, bfuse, gf, bef, mf,
         fused_codes = keep.tile([P, FUSED_PASSES, COLS], U32, align_bytes=64)
         fused_scales = keep.tile([P, FUSED_PASSES, COLS], U8, align_bytes=64)
 
-        def transpose_weights(raw, pairs):
+        def transpose_weights(raw, pairs, split=False):
             words = raw[:].bitcast(F32)
             grouped_pairs = []
             for pair in range(pairs):
@@ -144,9 +144,11 @@ def tile_afnb_pb_kernel(tc, context, high_feats, ww, bw, wf, bfuse, gf, bef, mf,
                 for q in range(4):
                     a, u = divmod(q, 2)
                     first = (2 * pair + a) * WORDS_PASS
-                    nc.tensor.transpose(
-                        flipped[:, q, :], words[:, first + u : first + WORDS_PASS : 2], identity[:]
-                    )
+                    if split:
+                        chosen = words[:, first + u * P : first + (u + 1) * P]
+                    else:
+                        chosen = words[:, first + u : first + WORDS_PASS : 2]
+                    nc.tensor.transpose(flipped[:, q, :], chosen, identity[:])
                 grouped = stage.tile([P, 2 * P * PACK], BF16, name="w_grouped", bufs=6, align_bytes=64)
                 nc.scalar.copy(
                     out=grouped[:].bitcast(F32).rearrange("p (a r u) -> p a r u", a=2, u=2),
@@ -162,8 +164,20 @@ def tile_afnb_pb_kernel(tc, context, high_feats, ww, bw, wf, bfuse, gf, bef, mf,
 
         wf_grouped = [None] * OUT_TILES
 
+        wf_split = [None] * OUT_TILES
+
+        def split_wf(m, copy):
+            wf_split[m] = stage.tile([P, C_FUSED], BF16, name="wf_split", bufs=2)
+            copy(
+                out=wf_split[m][:].bitcast(F32).rearrange("p (g u i) -> p g u i", u=2, i=P),
+                in_=wf_raw[m][:].bitcast(F32).rearrange("p (g i u) -> p g u i", u=2, i=P),
+            )
+
         def transpose_wf(m):
-            wf_grouped[m] = transpose_weights(wf_raw[m], FUSED_PASSES // 2)
+            if wf_split[m] is not None:
+                wf_grouped[m] = transpose_weights(wf_split[m], FUSED_PASSES // 2, split=True)
+            else:
+                wf_grouped[m] = transpose_weights(wf_raw[m], FUSED_PASSES // 2)
 
         def quantise_wf(m):
             quantise_weights(wf_grouped[m], wf_codes, wf_scales, m * FUSED_PASSES)
@@ -253,11 +267,26 @@ def tile_afnb_pb_kernel(tc, context, high_feats, ww, bw, wf, bfuse, gf, bef, mf,
                     in_=result[:, offset : offset + number],
                 )
 
+        short = (short_banks, "short")
+        sums = (sum_banks, "y_sum")
+        next_grouped = [None] * BLOCKS
+
+        def prepare_next(index, step):
+            if index + 1 == len(CHUNKS):
+                return
+            following = CHUNKS[index + 1]
+            for j in range(C_TILES_A_STEP * (step - FIRST_C_STEP), C_TILES_A_STEP * (step - FIRST_C_STEP + 1)):
+                if 0 <= j < MID_TILES:
+                    c_tile(j, *following, short)
+            block = step - FIRST_BLOCK_STEP
+            if 0 <= block < BLOCKS:
+                next_grouped[block] = regroup_block(block, *following)
+            if 0 <= block - 1 < BLOCKS:
+                quantise_block(block - 1, next_grouped[block - 1], *following)
+
         first_chunk = CHUNKS[0]
         gain = keep.tile([P, OUT_TILES], F32)
         shift = keep.tile([P, OUT_TILES], F32)
-        short = (short_banks, "short")
-        sums = (sum_banks, "y_sum")
 
         one = keep.tile([P, 1], F32)
         nc.vector.memset(one[:], 1.0)
@@ -285,40 +314,38 @@ def tile_afnb_pb_kernel(tc, context, high_feats, ww, bw, wf, bfuse, gf, bef, mf,
         for i in range(HALF):
             quantise_block(2 + i, grouped[1 + i], *first_chunk)
             grouped.append(regroup_block(3 + i, *first_chunk))
-            if i == 0:
+            if i == HALF - 1:
                 nc.vector.tensor_scalar_add(out=gain[:], in0=per_channel["vf"][:], scalar1=EPS)
                 nc.scalar.sqrt(out=gain[:], in_=gain[:])
                 nc.vector.tensor_sub(out=shift[:], in0=per_channel["bfuse"][:], in1=per_channel["mf"][:])
-            elif i == 1:
-                nc.vector.reciprocal(out=gain[:], in_=gain[:])
-            elif i == 2:
-                nc.vector.tensor_mul(out=gain[:], in0=gain[:], in1=per_channel["gf"][:])
-            else:
-                nc.vector.tensor_mul(out=shift[:], in0=shift[:], in1=gain[:])
-            quantise_wf(i + 2)
+            if i + 2 < HALF:
+                quantise_wf(i + 2)
             for m in range(len(y_sums), min(i + 2, HALF)):
                 y_sums[m] = sum_banks.tile([P, CHUNK], F32, name="y_sum")
                 y_passes(y_sums[m], m, range(MID_PASSES, MID_PASSES + i), *first_chunk)
             for m in y_sums:
                 y_passes(y_sums[m], m, (MID_PASSES + i,), *first_chunk)
-            if i + 3 < 6:
+            if i + 3 < HALF:
                 transpose_wf(i + 3)
+            if i in (1, 2):
+                split_wf(HALF + i - 1, nc.scalar.copy)
+            if i == HALF - 1:
+                transpose_wf(HALF)
+        nc.vector.reciprocal(out=gain[:], in_=gain[:])
+        nc.vector.tensor_mul(out=gain[:], in0=gain[:], in1=per_channel["gf"][:])
         quantise_block(6, grouped[5], *first_chunk)
+        nc.vector.tensor_mul(out=shift[:], in0=shift[:], in1=gain[:])
+        quantise_wf(HALF)
         nc.vector.tensor_add(out=shift[:], in0=shift[:], in1=per_channel["bef"][:])
         for m in range(HALF):
             y_passes(y_sums[m], m, range(MID_PASSES), *first_chunk)
             finish_tile(y_sums[m], m, *first_chunk)
-
-        def prepare_next(index, step):
-            if index + 1 == len(CHUNKS):
-                return
-            following = CHUNKS[index + 1]
-            for j in range(C_TILES_A_STEP * (step - FIRST_C_STEP), C_TILES_A_STEP * (step - FIRST_C_STEP + 1)):
-                if 0 <= j < MID_TILES:
-                    c_tile(j, *following, short)
-            block = step - FIRST_BLOCK_STEP
-            if 0 <= block < BLOCKS:
-                quantise_block(block, regroup_block(block, *following), *following)
+            if m == 1:
+                split_wf(HALF + 2, nc.vector.tensor_copy)
+                transpose_wf(HALF + 1)
+                quantise_wf(HALF + 1)
+        prepare_next(0, FIRST_BLOCK_STEP)
+        split_wf(HALF + 3, nc.vector.tensor_copy)
 
         for index, (col0, width) in enumerate(CHUNKS):
             for half in range(1 if index == 0 else 0, 2):

@@ -9,6 +9,7 @@ U32 = mybir.dt.uint32
 U8 = mybir.dt.uint8
 FP8X4 = mybir.dt.float8_e4m3fn_x4
 ACT = mybir.ActivationFunctionType
+ALU = mybir.AluOpType
 
 P = 128
 PACK = 4
@@ -239,7 +240,7 @@ def tile_afnb_pb_kernel(tc, context, high_feats, ww, bw, wf, bfuse, gf, bef, mf,
                 bias=bw_bf[:, j : j + 1], scale=1.0,
             )
 
-        def y_passes(y_sum, m, passes, col0, width):
+        def y_passes(y_sum, m, passes, col0, width, last=MID_PASSES - 1):
             cols = slice(col0, col0 + width)
             for g in passes:
                 w_cols = slice((m * FUSED_PASSES + g) * P, (m * FUSED_PASSES + g + 1) * P)
@@ -250,7 +251,7 @@ def tile_afnb_pb_kernel(tc, context, high_feats, ww, bw, wf, bfuse, gf, bef, mf,
                     rhs=fused_codes[:, g, cols].bitcast(FP8X4),
                     rhs_scale=fused_scales[:, g, cols],
                     start=(g == MID_PASSES),
-                    stop=(g == MID_PASSES - 1),
+                    stop=(g == last),
                 )
 
         def finish_tile(y_sum, m, col0, width):
@@ -288,14 +289,24 @@ def tile_afnb_pb_kernel(tc, context, high_feats, ww, bw, wf, bfuse, gf, bef, mf,
         gain = keep.tile([P, OUT_TILES], F32)
         shift = keep.tile([P, OUT_TILES], F32)
 
+        power = keep.tile([P, OUT_TILES], F32)
+        nc.gpsimd.memset(power[:], -0.5)
+        nc.gpsimd.tensor_scalar_add(out=gain[:], in0=per_channel["vf"][:], scalar1=EPS)
+        nc.gpsimd.tensor_tensor(out=gain[:], in0=gain[:], in1=power[:], op=ALU.pow)
+        nc.gpsimd.tensor_mul(out=gain[:], in0=gain[:], in1=per_channel["gf"][:])
+        nc.gpsimd.tensor_sub(out=shift[:], in0=per_channel["bfuse"][:], in1=per_channel["mf"][:])
+        nc.gpsimd.tensor_mul(out=shift[:], in0=shift[:], in1=gain[:])
+        nc.gpsimd.tensor_add(out=shift[:], in0=shift[:], in1=per_channel["bef"][:])
+
         one = keep.tile([P, 1], F32)
         nc.vector.memset(one[:], 1.0)
-        nc.scalar.sqrt(out=one[:], in_=one[:])
+        nc.scalar.copy(out=one[:], in_=one[:])
 
+        LAST = FUSED_PASSES - 1
         ww_grouped = [transpose_weights(ww_raw[g], PACK // 2) for g in range(MID_PASSES)]
-        grouped_ctx = regroup_block(0, *first_chunk)
+        grouped = {0: regroup_block(0, *first_chunk)}
         quantise_weights(ww_grouped[0], ww_codes, ww_scales, 0)
-        quantise_block(0, grouped_ctx, *first_chunk)
+        quantise_block(0, grouped[0], *first_chunk)
         quantise_weights(ww_grouped[1], ww_codes, ww_scales, PACK)
         for j in range(PACK):
             c_tile(j, *first_chunk, sums)
@@ -304,48 +315,52 @@ def tile_afnb_pb_kernel(tc, context, high_feats, ww, bw, wf, bfuse, gf, bef, mf,
         for j in range(PACK, MID_TILES):
             c_tile(j, *first_chunk, sums)
         transpose_wf(2)
-
-        y_sums = {}
-        grouped = [regroup_block(1, *first_chunk)]
+        grouped[1] = regroup_block(1, *first_chunk)
+        quantise_block(1, grouped[1], *first_chunk)
         quantise_wf(0)
-        quantise_block(1, grouped[0], *first_chunk)
-        grouped.append(regroup_block(2, *first_chunk))
+        grouped[5] = regroup_block(5, *first_chunk)
         quantise_wf(1)
-        for i in range(HALF):
-            quantise_block(2 + i, grouped[1 + i], *first_chunk)
-            grouped.append(regroup_block(3 + i, *first_chunk))
-            if i == HALF - 1:
-                nc.vector.tensor_scalar_add(out=gain[:], in0=per_channel["vf"][:], scalar1=EPS)
-                nc.scalar.sqrt(out=gain[:], in_=gain[:])
-                nc.vector.tensor_sub(out=shift[:], in0=per_channel["bfuse"][:], in1=per_channel["mf"][:])
-            if i + 2 < HALF:
-                quantise_wf(i + 2)
-            for m in range(len(y_sums), min(i + 2, HALF)):
+        grouped[2] = regroup_block(2, *first_chunk)
+        quantise_block(5, grouped[5], *first_chunk)
+        y_sums = {}
+
+        def open_tiles(count, passes):
+            for m in range(len(y_sums), count):
                 y_sums[m] = sum_banks.tile([P, CHUNK], F32, name="y_sum")
-                y_passes(y_sums[m], m, range(MID_PASSES, MID_PASSES + i), *first_chunk)
+                y_passes(y_sums[m], m, passes, *first_chunk, LAST)
+
+        def block_passes(g):
             for m in y_sums:
-                y_passes(y_sums[m], m, (MID_PASSES + i,), *first_chunk)
-            if i + 3 < HALF:
-                transpose_wf(i + 3)
-            if i in (1, 2):
-                split_wf(HALF + i - 1, nc.scalar.copy)
-            if i == HALF - 1:
-                transpose_wf(HALF)
-        nc.vector.reciprocal(out=gain[:], in_=gain[:])
-        nc.vector.tensor_mul(out=gain[:], in0=gain[:], in1=per_channel["gf"][:])
-        quantise_block(6, grouped[5], *first_chunk)
-        nc.vector.tensor_mul(out=shift[:], in0=shift[:], in1=gain[:])
-        quantise_wf(HALF)
-        nc.vector.tensor_add(out=shift[:], in0=shift[:], in1=per_channel["bef"][:])
+                y_passes(y_sums[m], m, (g,), *first_chunk, LAST)
+
+        open_tiles(2, (2, 0))
+        transpose_wf(3)
+        quantise_wf(2)
+        quantise_block(2, grouped[2], *first_chunk)
+        grouped[6] = regroup_block(6, *first_chunk)
+        open_tiles(3, (2, 0))
+        block_passes(3)
+        quantise_wf(3)
+        quantise_block(6, grouped[6], *first_chunk)
+        grouped[3] = regroup_block(3, *first_chunk)
+        open_tiles(4, (2, 0, 3))
+        split_wf(4, nc.scalar.copy)
+        split_wf(5, nc.scalar.copy)
+        block_passes(1)
+        transpose_wf(4)
+        grouped[4] = regroup_block(4, *first_chunk)
+        quantise_block(3, grouped[3], *first_chunk)
+        block_passes(4)
+        transpose_wf(5)
+        quantise_block(4, grouped[4], *first_chunk)
+        quantise_wf(4)
+        split_wf(6, nc.vector.tensor_copy)
         for m in range(HALF):
-            y_passes(y_sums[m], m, range(MID_PASSES), *first_chunk)
+            y_passes(y_sums[m], m, (LAST,), *first_chunk, LAST)
             finish_tile(y_sums[m], m, *first_chunk)
-            if m == 1:
-                split_wf(HALF + 2, nc.vector.tensor_copy)
-                transpose_wf(HALF + 1)
-                quantise_wf(HALF + 1)
         prepare_next(0, FIRST_BLOCK_STEP)
-        split_wf(HALF + 3, nc.vector.tensor_copy)
+        quantise_wf(5)
+        split_wf(7, nc.vector.tensor_copy)
 
         for index, (col0, width) in enumerate(CHUNKS):
             for half in range(1 if index == 0 else 0, 2):

@@ -9,7 +9,6 @@ U32 = mybir.dt.uint32
 U8 = mybir.dt.uint8
 FP8X4 = mybir.dt.float8_e4m3fn_x4
 ACT = mybir.ActivationFunctionType
-ALU = mybir.AluOpType
 
 P = 128
 PACK = 4
@@ -70,7 +69,9 @@ def tile_afnb_pb_kernel(tc, context, high_feats, ww, bw, wf, bfuse, gf, bef, mf,
 
         def load_activations(rows, name):
             raw = keep.tile([P, PACK, PIXELS], BF16, name=name)
-            nc.sync.dma_start(out=raw[:], in_=rows.rearrange("(p t) h w -> p t (h w)", t=PACK))
+            nc.sync.dma_start(
+                out=raw[:].rearrange("p t n -> p (t n)"), in_=rows.rearrange("(p t) h w -> p (t h w)", t=PACK)
+            )
             return raw
 
         ctx_raw = [None] * IMAGES
@@ -108,11 +109,13 @@ def tile_afnb_pb_kernel(tc, context, high_feats, ww, bw, wf, bfuse, gf, bef, mf,
             )
 
         def load_norm():
-            for name, vector in (("vf", vf), ("gf", gf), ("bfuse", bfuse), ("mf", mf), ("bef", bef)):
+            for name, vector in (("gf", gf), ("bfuse", bfuse), ("mf", mf), ("bef", bef)):
                 per_channel[name] = keep.tile([P, OUT_TILES], BF16, name=name + "_bf")
                 nc.sync.dma_start(out=per_channel[name][:], in_=vector.rearrange("(p m) -> p m", m=OUT_TILES))
 
         load_bw()
+        per_channel["vf"] = keep.tile([P, OUT_TILES], BF16, name="vf_bf")
+        nc.scalar.dma_start(out=per_channel["vf"][:], in_=vf.rearrange("(p m) -> p m", m=OUT_TILES))
         load_ww(0)
         load_context(0)
         load_ww(1)
@@ -289,18 +292,12 @@ def tile_afnb_pb_kernel(tc, context, high_feats, ww, bw, wf, bfuse, gf, bef, mf,
         gain = keep.tile([P, OUT_TILES], F32)
         shift = keep.tile([P, OUT_TILES], F32)
 
-        power = keep.tile([P, OUT_TILES], F32)
-        nc.gpsimd.memset(power[:], -0.5)
-        nc.gpsimd.tensor_scalar_add(out=gain[:], in0=per_channel["vf"][:], scalar1=EPS)
-        nc.gpsimd.tensor_tensor(out=gain[:], in0=gain[:], in1=power[:], op=ALU.pow)
-        nc.gpsimd.tensor_mul(out=gain[:], in0=gain[:], in1=per_channel["gf"][:])
-        nc.gpsimd.tensor_sub(out=shift[:], in0=per_channel["bfuse"][:], in1=per_channel["mf"][:])
-        nc.gpsimd.tensor_mul(out=shift[:], in0=shift[:], in1=gain[:])
-        nc.gpsimd.tensor_add(out=shift[:], in0=shift[:], in1=per_channel["bef"][:])
-
         one = keep.tile([P, 1], F32)
         nc.vector.memset(one[:], 1.0)
-        nc.scalar.copy(out=one[:], in_=one[:])
+        nc.scalar.sqrt(out=one[:], in_=one[:])
+        nc.vector.tensor_scalar_add(out=gain[:], in0=per_channel["vf"][:], scalar1=EPS)
+        nc.scalar.sqrt(out=gain[:], in_=gain[:])
+        nc.vector.reciprocal(out=gain[:], in_=gain[:])
 
         LAST = FUSED_PASSES - 1
         ww_grouped = [transpose_weights(ww_raw[g], PACK // 2) for g in range(MID_PASSES)]
@@ -344,16 +341,18 @@ def tile_afnb_pb_kernel(tc, context, high_feats, ww, bw, wf, bfuse, gf, bef, mf,
         quantise_block(6, grouped[6], *first_chunk)
         grouped[3] = regroup_block(3, *first_chunk)
         open_tiles(4, (2, 0, 3))
-        split_wf(4, nc.scalar.copy)
-        split_wf(5, nc.scalar.copy)
         block_passes(1)
         transpose_wf(4)
         grouped[4] = regroup_block(4, *first_chunk)
         quantise_block(3, grouped[3], *first_chunk)
         block_passes(4)
         transpose_wf(5)
+        nc.vector.tensor_sub(out=shift[:], in0=per_channel["bfuse"][:], in1=per_channel["mf"][:])
         quantise_block(4, grouped[4], *first_chunk)
         quantise_wf(4)
+        nc.vector.tensor_mul(out=gain[:], in0=gain[:], in1=per_channel["gf"][:])
+        nc.vector.tensor_mul(out=shift[:], in0=shift[:], in1=gain[:])
+        nc.vector.tensor_add(out=shift[:], in0=shift[:], in1=per_channel["bef"][:])
         split_wf(6, nc.vector.tensor_copy)
         for m in range(HALF):
             y_passes(y_sums[m], m, (LAST,), *first_chunk, LAST)

@@ -123,11 +123,11 @@ def tile_afnb_pb_kernel(tc, context, high_feats, ww, bw, wf, bfuse, gf, bef, mf,
         for i in range(HIGH_PASSES):
             load_high(0, i)
             load_wf(i + 1)
-        for m in range(HIGH_PASSES + 1, OUT_TILES):
-            load_wf(m)
-            if m == HIGH_PASSES + 1:
-                load_norm()
+        load_wf(5)
+        load_norm()
+        load_wf(6)
         load_context(1)
+        load_wf(7)
         for h in range(HIGH_PASSES):
             load_high(1, h)
 

@@ -123,8 +123,8 @@ def tile_afnb_pb_kernel(tc, context, high_feats, ww, bw, wf, bfuse, gf, bef, mf,
         for i in range(HIGH_PASSES):
             load_high(0, i)
             load_wf(i + 1)
-        load_wf(5)
         load_norm()
+        load_wf(5)
         load_wf(6)
         load_context(1)
         load_wf(7)
@@ -142,7 +142,7 @@ def tile_afnb_pb_kernel(tc, context, high_feats, ww, bw, wf, bfuse, gf, bef, mf,
 
         def transpose_weights(raw, pairs, split=False):
             words = raw[:].bitcast(F32)
-            grouped_pairs = []
+            grouped = stage.tile([P, C_FUSED], BF16, name="w_grouped", bufs=2, align_bytes=64)
             for pair in range(pairs):
                 flipped = short_banks.tile([P, 4, P], F32, name="short")
                 for q in range(4):
@@ -153,18 +153,22 @@ def tile_afnb_pb_kernel(tc, context, high_feats, ww, bw, wf, bfuse, gf, bef, mf,
                     else:
                         chosen = words[:, first + u : first + WORDS_PASS : 2]
                     nc.tensor.transpose(flipped[:, q, :], chosen, identity[:])
-                grouped = stage.tile([P, 2 * P * PACK], BF16, name="w_grouped", bufs=6, align_bytes=64)
+                part = slice(pair * 2 * K_PASS, (pair + 1) * 2 * K_PASS)
                 nc.scalar.copy(
-                    out=grouped[:].bitcast(F32).rearrange("p (a r u) -> p a r u", a=2, u=2),
+                    out=grouped[:, part].bitcast(F32).rearrange("p (a r u) -> p a r u", a=2, u=2),
                     in_=flipped[:].rearrange("p (a u) r -> p a r u", u=2),
                 )
-                grouped_pairs.append(grouped)
-            return grouped_pairs
+            return grouped
 
-        def quantise_weights(grouped_pairs, codes, scales, first_operand):
-            for pair, grouped in enumerate(grouped_pairs):
-                cols = slice((first_operand + 2 * pair) * P, (first_operand + 2 * pair + 2) * P)
-                nc.vector.quantize_mx(out=codes[:, cols].bitcast(FP8X4), scales=scales[:, cols], in_=grouped[:])
+        def quantise_weights(grouped, codes, scales, first_operand, operands):
+            for done in range(0, operands, 4):
+                count = min(4, operands - done)
+                cols = slice((first_operand + done) * P, (first_operand + done + count) * P)
+                nc.vector.quantize_mx(
+                    out=codes[:, cols].bitcast(FP8X4),
+                    scales=scales[:, cols],
+                    in_=grouped[:, done * K_PASS : (done + count) * K_PASS],
+                )
 
         wf_grouped = [None] * OUT_TILES
 
@@ -184,12 +188,12 @@ def tile_afnb_pb_kernel(tc, context, high_feats, ww, bw, wf, bfuse, gf, bef, mf,
                 wf_grouped[m] = transpose_weights(wf_raw[m], FUSED_PASSES // 2)
 
         def quantise_wf(m):
-            quantise_weights(wf_grouped[m], wf_codes, wf_scales, m * FUSED_PASSES)
+            quantise_weights(wf_grouped[m], wf_codes, wf_scales, m * FUSED_PASSES, FUSED_PASSES)
 
-        def regroup(sources):
+        def regroup(sources, copy):
             grouped = stage.tile([P, CHUNK, PACK], BF16, name="a_grouped", align_bytes=64)
             for rows, first, number, offset in sources:
-                nc.vector.tensor_copy(
+                copy(
                     out=grouped[:, offset : offset + number, :].rearrange("p (c i) t -> p c t i", i=4),
                     in_=rows[:, :, first : first + number].rearrange("p t (c i) -> p c t i", i=4),
                 )
@@ -204,15 +208,16 @@ def tile_afnb_pb_kernel(tc, context, high_feats, ww, bw, wf, bfuse, gf, bef, mf,
 
         c_rows = [None] * MID_PASSES
 
-        def regroup_block(block, col0, width):
+        def regroup_block(block, col0, width, copy=nc.vector.tensor_copy):
             pieces = image_pieces(col0, width)
             if block == 0:
-                return regroup([(ctx_raw[image], first, number, offset) for image, first, number, offset in pieces])
+                return regroup([(ctx_raw[image], first, number, offset) for image, first, number, offset in pieces], copy)
             if block <= HIGH_PASSES:
                 return regroup(
-                    [(high_raw[image][block - 1], first, number, offset) for image, first, number, offset in pieces]
+                    [(high_raw[image][block - 1], first, number, offset) for image, first, number, offset in pieces],
+                    copy,
                 )
-            return regroup([(c_rows[block - 1 - HIGH_PASSES], 0, width, 0)])
+            return regroup([(c_rows[block - 1 - HIGH_PASSES], 0, width, 0)], copy)
 
         def quantise_block(block, grouped, col0, width):
             cols = slice(col0, col0 + width)
@@ -295,16 +300,16 @@ def tile_afnb_pb_kernel(tc, context, high_feats, ww, bw, wf, bfuse, gf, bef, mf,
         one = keep.tile([P, 1], F32)
         nc.vector.memset(one[:], 1.0)
         nc.scalar.sqrt(out=one[:], in_=one[:])
-        nc.vector.tensor_scalar_add(out=gain[:], in0=per_channel["vf"][:], scalar1=EPS)
-        nc.scalar.sqrt(out=gain[:], in_=gain[:])
-        nc.vector.reciprocal(out=gain[:], in_=gain[:])
 
         LAST = FUSED_PASSES - 1
         ww_grouped = [transpose_weights(ww_raw[g], PACK // 2) for g in range(MID_PASSES)]
         grouped = {0: regroup_block(0, *first_chunk)}
-        quantise_weights(ww_grouped[0], ww_codes, ww_scales, 0)
+        quantise_weights(ww_grouped[0], ww_codes, ww_scales, 0, PACK)
+        nc.vector.tensor_scalar_add(out=gain[:], in0=per_channel["vf"][:], scalar1=EPS)
         quantise_block(0, grouped[0], *first_chunk)
-        quantise_weights(ww_grouped[1], ww_codes, ww_scales, PACK)
+        nc.scalar.sqrt(out=gain[:], in_=gain[:])
+        quantise_weights(ww_grouped[1], ww_codes, ww_scales, PACK, PACK)
+        nc.vector.reciprocal(out=gain[:], in_=gain[:])
         for j in range(PACK):
             c_tile(j, *first_chunk, sums)
         transpose_wf(0)
@@ -314,11 +319,11 @@ def tile_afnb_pb_kernel(tc, context, high_feats, ww, bw, wf, bfuse, gf, bef, mf,
         transpose_wf(2)
         grouped[1] = regroup_block(1, *first_chunk)
         quantise_block(1, grouped[1], *first_chunk)
-        quantise_wf(0)
         grouped[5] = regroup_block(5, *first_chunk)
-        quantise_wf(1)
-        grouped[2] = regroup_block(2, *first_chunk)
+        quantise_wf(0)
         quantise_block(5, grouped[5], *first_chunk)
+        grouped[2] = regroup_block(2, *first_chunk)
+        quantise_wf(1)
         y_sums = {}
 
         def open_tiles(count, passes):
@@ -330,28 +335,31 @@ def tile_afnb_pb_kernel(tc, context, high_feats, ww, bw, wf, bfuse, gf, bef, mf,
             for m in y_sums:
                 y_passes(y_sums[m], m, (g,), *first_chunk, LAST)
 
-        open_tiles(2, (2, 0))
+        open_tiles(2, (2,))
         transpose_wf(3)
-        quantise_wf(2)
+        block_passes(0)
         quantise_block(2, grouped[2], *first_chunk)
         grouped[6] = regroup_block(6, *first_chunk)
+        quantise_wf(2)
         open_tiles(3, (2, 0))
         block_passes(3)
-        quantise_wf(3)
         quantise_block(6, grouped[6], *first_chunk)
+        quantise_wf(3)
         grouped[3] = regroup_block(3, *first_chunk)
+        split_wf(4, nc.vector.tensor_copy)
         open_tiles(4, (2, 0, 3))
         block_passes(1)
+        grouped[4] = regroup_block(4, *first_chunk, nc.scalar.copy)
         transpose_wf(4)
-        grouped[4] = regroup_block(4, *first_chunk)
         quantise_block(3, grouped[3], *first_chunk)
         block_passes(4)
+        split_wf(5, nc.vector.tensor_copy)
         transpose_wf(5)
+        nc.vector.tensor_mul(out=gain[:], in0=gain[:], in1=per_channel["gf"][:])
         nc.vector.tensor_sub(out=shift[:], in0=per_channel["bfuse"][:], in1=per_channel["mf"][:])
         quantise_block(4, grouped[4], *first_chunk)
-        quantise_wf(4)
-        nc.vector.tensor_mul(out=gain[:], in0=gain[:], in1=per_channel["gf"][:])
         nc.vector.tensor_mul(out=shift[:], in0=shift[:], in1=gain[:])
+        quantise_wf(4)
         nc.vector.tensor_add(out=shift[:], in0=shift[:], in1=per_channel["bef"][:])
         split_wf(6, nc.vector.tensor_copy)
         for m in range(HALF):
@@ -367,10 +375,11 @@ def tile_afnb_pb_kernel(tc, context, high_feats, ww, bw, wf, bfuse, gf, bef, mf,
                 y_sums = {}
                 for m in tiles:
                     prepare_next(index, 2 * half * HALF + m % HALF)
+                    if index == 0 and m + WF_AHEAD < OUT_TILES:
+                        transpose_wf(m + WF_AHEAD)
                     y_sums[m] = sum_banks.tile([P, CHUNK], F32, name="y_sum")
                     y_passes(y_sums[m], m, range(MID_PASSES, FUSED_PASSES), col0, width)
                     if index == 0 and m + WF_AHEAD < OUT_TILES:
-                        transpose_wf(m + WF_AHEAD)
                         quantise_wf(m + WF_AHEAD)
                 for m in tiles:
                     prepare_next(index, (2 * half + 1) * HALF + m % HALF)

from contextlib import ExitStack

import concourse.mybir as mybir
from concourse.masks import make_identity

F32 = mybir.dt.float32
BF16 = mybir.dt.bfloat16
U32 = mybir.dt.uint32
U8 = mybir.dt.uint8
FP8X4 = mybir.dt.float8_e4m3fn_x4
ACT = mybir.ActivationFunctionType

P = 128
PACK = 4
K_PASS = P * PACK
WORDS_PASS = K_PASS // 2

IMAGES = 2
PIXELS = 24 * 24
COLS = IMAGES * PIXELS
C_CTX = 512
C_MID = 1024
C_HIGH = 2048
C_FUSED = C_MID + C_HIGH
C_OUT = 1024
EPS = 1e-5

MID_TILES = C_MID // P
MID_PASSES = C_MID // K_PASS
HIGH_PASSES = C_HIGH // K_PASS
FUSED_PASSES = MID_PASSES + HIGH_PASSES
OUT_TILES = C_OUT // P
HALF = OUT_TILES // 2

CHUNK = 512
CHUNKS = ((0, 512), (512, 512), (1024, 128))
WF_AHEAD = 2

STEPS = 4 * HALF
FIRST_BLOCK_STEP = STEPS // 2 - 1
BLOCKS = 1 + HIGH_PASSES + MID_PASSES
FIRST_C_STEP = FIRST_BLOCK_STEP + 3
C_TILES_A_STEP = 2

FLOPS = 2 * COLS * (C_MID * C_CTX + C_OUT * C_FUSED)


def image_pieces(col0, width):
    pieces = []
    for image in range(IMAGES):
        lo = max(col0, image * PIXELS)
        hi = min(col0 + width, (image + 1) * PIXELS)
        if lo < hi:
            pieces.append((image, lo - image * PIXELS, hi - lo, lo - col0))
    return pieces


def tile_afnb_pb_kernel(tc, context, high_feats, ww, bw, wf, bfuse, gf, bef, mf, vf, out):
    nc = tc.nc
    with ExitStack() as ctx:
        ctx.enter_context(tc.manual_schedule())
        keep = ctx.enter_context(tc.tile_pool(name="keep", bufs=1))
        stage = ctx.enter_context(tc.tile_pool(name="stage", bufs=4))
        short_banks = ctx.enter_context(tc.psum_pool(name="short_banks", bufs=4))
        sum_banks = ctx.enter_context(tc.psum_pool(name="sum_banks", bufs=HALF))

        identity = keep.tile([P, P], F32)
        make_identity(nc, identity[:])

        def load_activations(rows, name):
            raw = keep.tile([P, PACK, PIXELS], BF16, name=name)
            nc.sync.dma_start(
                out=raw[:].rearrange("p t n -> p (t n)"), in_=rows.rearrange("(p t) h w -> p (t h w)", t=PACK)
            )
            return raw

        ctx_raw = [None] * IMAGES
        high_raw = [[None] * HIGH_PASSES for image in range(IMAGES)]
        wf_raw = [None] * OUT_TILES

        def load_context(image):
            ctx_raw[image] = load_activations(context[image], "ctx_raw%d" % image)

        def load_high(image, h):
            high_raw[image][h] = load_activations(
                high_feats[image, h * K_PASS : (h + 1) * K_PASS], "high_raw%d_%d" % (image, h)
            )

        def load_wf(m):
            wf_raw[m] = keep.tile([P, C_FUSED], BF16, name="wf_raw%d" % m)
            nc.sync.dma_start(out=wf_raw[m][:], in_=wf.rearrange("(p m) k -> p m k", m=OUT_TILES)[:, m, :])

        ww_raw = [None] * MID_PASSES

        def load_ww(g):
            ww_raw[g] = keep.tile([P, PACK * C_CTX], BF16, name="ww_raw%d" % g)
            nc.sync.dma_start(
                out=ww_raw[g][:],
                in_=ww[g * K_PASS : (g + 1) * K_PASS, :].rearrange("(p t) k -> p (t k)", t=PACK),
            )

        bw_bf = keep.tile([P, MID_TILES], BF16)
        per_channel = {}

        def load_bw():
            nc.scalar.dma_start(
                out=bw_bf[:].rearrange("p (g t) -> p g t", t=PACK),
                in_=bw.rearrange("(g p t) -> p g t", p=P, t=PACK),
            )

        def load_norm():
            for name, vector in (("gf", gf), ("bfuse", bfuse), ("mf", mf), ("bef", bef)):
                per_channel[name] = keep.tile([P, OUT_TILES], BF16, name=name + "_bf")
                nc.sync.dma_start(out=per_channel[name][:], in_=vector.rearrange("(p m) -> p m", m=OUT_TILES))

        load_bw()
        per_channel["vf"] = keep.tile([P, OUT_TILES], BF16, name="vf_bf")
        nc.scalar.dma_start(out=per_channel["vf"][:], in_=vf.rearrange("(p m) -> p m", m=OUT_TILES))
        load_ww(0)
        load_context(0)
        load_ww(1)
        load_wf(0)
        for i in range(HIGH_PASSES):
            load_high(0, i)
            load_wf(i + 1)
        load_norm()
        load_wf(5)
        load_wf(6)
        load_context(1)
        load_wf(7)
        for h in range(HIGH_PASSES):
            load_high(1, h)

        ww_codes = keep.tile([P, MID_TILES * P], U32, align_bytes=64)
        ww_scales = keep.tile([P, MID_TILES * P], U8, align_bytes=64)
        wf_codes = keep.tile([P, OUT_TILES * FUSED_PASSES * P], U32, align_bytes=64)
        wf_scales = keep.tile([P, OUT_TILES * FUSED_PASSES * P], U8, align_bytes=64)
        ctx_codes = keep.tile([P, COLS], U32, align_bytes=64)
        ctx_scales = keep.tile([P, COLS], U8, align_bytes=64)
        fused_codes = keep.tile([P, FUSED_PASSES, COLS], U32, align_bytes=64)
        fused_scales = keep.tile([P, FUSED_PASSES, COLS], U8, align_bytes=64)

        def transpose_weights(raw, pairs, split=False):
            words = raw[:].bitcast(F32)
            grouped = stage.tile([P, C_FUSED], BF16, name="w_grouped", bufs=2, align_bytes=64)
            for pair in range(pairs):
                flipped = short_banks.tile([P, 4, P], F32, name="short")
                for q in range(4):
                    a, u = divmod(q, 2)
                    first = (2 * pair + a) * WORDS_PASS
                    if split:
                        chosen = words[:, first + u * P : first + (u + 1) * P]
                    else:
                        chosen = words[:, first + u : first + WORDS_PASS : 2]
                    nc.tensor.transpose(flipped[:, q, :], chosen, identity[:])
                part = slice(pair * 2 * K_PASS, (pair + 1) * 2 * K_PASS)
                nc.scalar.copy(
                    out=grouped[:, part].bitcast(F32).rearrange("p (a r u) -> p a r u", a=2, u=2),
                    in_=flipped[:].rearrange("p (a u) r -> p a r u", u=2),
                )
            return grouped

        def quantise_weights(grouped, codes, scales, first_operand, operands):
            for done in range(0, operands, 4):
                count = min(4, operands - done)
                cols = slice((first_operand + done) * P, (first_operand + done + count) * P)
                nc.vector.quantize_mx(
                    out=codes[:, cols].bitcast(FP8X4),
                    scales=scales[:, cols],
                    in_=grouped[:, done * K_PASS : (done + count) * K_PASS],
                )

        wf_grouped = [None] * OUT_TILES

        wf_split = [None] * OUT_TILES

        def split_wf(m, copy):
            wf_split[m] = stage.tile([P, C_FUSED], BF16, name="wf_split", bufs=2)
            copy(
                out=wf_split[m][:].bitcast(F32).rearrange("p (g u i) -> p g u i", u=2, i=P),
                in_=wf_raw[m][:].bitcast(F32).rearrange("p (g i u) -> p g u i", u=2, i=P),
            )

        def transpose_wf(m):
            if wf_split[m] is not None:
                wf_grouped[m] = transpose_weights(wf_split[m], FUSED_PASSES // 2, split=True)
            else:
                wf_grouped[m] = transpose_weights(wf_raw[m], FUSED_PASSES // 2)

        def quantise_wf(m):
            quantise_weights(wf_grouped[m], wf_codes, wf_scales, m * FUSED_PASSES, FUSED_PASSES)

        def regroup(sources, copy):
            grouped = stage.tile([P, CHUNK, PACK], BF16, name="a_grouped", align_bytes=64)
            for rows, first, number, offset in sources:
                copy(
                    out=grouped[:, offset : offset + number, :].rearrange("p (c i) t -> p c t i", i=4),
                    in_=rows[:, :, first : first + number].rearrange("p t (c i) -> p c t i", i=4),
                )
            return grouped

        def quantise(grouped, width, codes, scales):
            nc.vector.quantize_mx(
                out=codes.bitcast(FP8X4),
                scales=scales,
                in_=grouped[:, :width, :].rearrange("p c t -> p (c t)"),
            )

        c_rows = [None] * MID_PASSES

        def regroup_block(block, col0, width, copy=nc.vector.tensor_copy):
            pieces = image_pieces(col0, width)
            if block == 0:
                return regroup([(ctx_raw[image], first, number, offset) for image, first, number, offset in pieces], copy)
            if block <= HIGH_PASSES:
                return regroup(
                    [(high_raw[image][block - 1], first, number, offset) for image, first, number, offset in pieces],
                    copy,
                )
            return regroup([(c_rows[block - 1 - HIGH_PASSES], 0, width, 0)], copy)

        def quantise_block(block, grouped, col0, width):
            cols = slice(col0, col0 + width)
            if block == 0:
                quantise(grouped, width, ctx_codes[:, cols], ctx_scales[:, cols])
            else:
                g = MID_PASSES + block - 1 if block <= HIGH_PASSES else block - 1 - HIGH_PASSES
                quantise(grouped, width, fused_codes[:, g, cols], fused_scales[:, g, cols])

        def c_tile(j, col0, width, banks):
            cols = slice(col0, col0 + width)
            g, t = divmod(j, PACK)
            if t == 0:
                c_rows[g] = stage.tile([P, PACK, CHUNK], BF16, name="c_rows", bufs=MID_PASSES)
            pool, name = banks
            c_sum = pool.tile([P, CHUNK], F32, name=name)
            nc.tensor.matmul_mx(
                out=c_sum[:, :width],
                lhsT=ww_codes[:, j * P : (j + 1) * P].bitcast(FP8X4),
                lhsT_scale=ww_scales[:, j * P : (j + 1) * P],
                rhs=ctx_codes[:, cols].bitcast(FP8X4),
                rhs_scale=ctx_scales[:, cols],
                start=True,
                stop=True,
            )
            nc.scalar.activation(
                out=c_rows[g][:, t, :width], in_=c_sum[:, :width], func=ACT.Identity,
                bias=bw_bf[:, j : j + 1], scale=1.0,
            )

        def y_passes(y_sum, m, passes, col0, width, last=MID_PASSES - 1):
            cols = slice(col0, col0 + width)
            for g in passes:
                w_cols = slice((m * FUSED_PASSES + g) * P, (m * FUSED_PASSES + g + 1) * P)
                nc.tensor.matmul_mx(
                    out=y_sum[:, :width],
                    lhsT=wf_codes[:, w_cols].bitcast(FP8X4),
                    lhsT_scale=wf_scales[:, w_cols],
                    rhs=fused_codes[:, g, cols].bitcast(FP8X4),
                    rhs_scale=fused_scales[:, g, cols],
                    start=(g == MID_PASSES),
                    stop=(g == last),
                )

        def finish_tile(y_sum, m, col0, width):
            result = stage.tile(
                [P, width], F32, name="result%d" % width, bufs=(HALF if width == CHUNK else OUT_TILES)
            )
            nc.scalar.activation(
                out=result[:, :width], in_=y_sum[:, :width], func=ACT.Identity,
                bias=shift[:, m : m + 1], scale=gain[:, m : m + 1],
            )
            for image, first, number, offset in image_pieces(col0, width):
                nc.sync.dma_start(
                    out=out[image].rearrange("(p m) h w -> p m (h w)", m=OUT_TILES)[:, m, first : first + number],
                    in_=result[:, offset : offset + number],
                )

        short = (short_banks, "short")
        sums = (sum_banks, "y_sum")
        next_grouped = [None] * BLOCKS

        def prepare_next(index, step):
            if index + 1 == len(CHUNKS):
                return
            following = CHUNKS[index + 1]
            for j in range(C_TILES_A_STEP * (step - FIRST_C_STEP), C_TILES_A_STEP * (step - FIRST_C_STEP + 1)):
                if 0 <= j < MID_TILES:
                    c_tile(j, *following, short)
            block = step - FIRST_BLOCK_STEP
            if 0 <= block < BLOCKS:
                next_grouped[block] = regroup_block(block, *following)
            if 0 <= block - 1 < BLOCKS:
                quantise_block(block - 1, next_grouped[block - 1], *following)

        first_chunk = CHUNKS[0]
        gain = keep.tile([P, OUT_TILES], F32)
        shift = keep.tile([P, OUT_TILES], F32)

        one = keep.tile([P, 1], F32)
        nc.vector.memset(one[:], 1.0)
        nc.scalar.sqrt(out=one[:], in_=one[:])

        LAST = FUSED_PASSES - 1
        ww_grouped = [transpose_weights(ww_raw[g], PACK // 2) for g in range(MID_PASSES)]
        grouped = {0: regroup_block(0, *first_chunk)}
        quantise_weights(ww_grouped[0], ww_codes, ww_scales, 0, PACK)
        nc.vector.tensor_scalar_add(out=gain[:], in0=per_channel["vf"][:], scalar1=EPS)
        quantise_block(0, grouped[0], *first_chunk)
        nc.scalar.sqrt(out=gain[:], in_=gain[:])
        quantise_weights(ww_grouped[1], ww_codes, ww_scales, PACK, PACK)
        nc.vector.reciprocal(out=gain[:], in_=gain[:])
        for j in range(PACK):
            c_tile(j, *first_chunk, sums)
        transpose_wf(0)
        transpose_wf(1)
        for j in range(PACK, MID_TILES):
            c_tile(j, *first_chunk, sums)
        transpose_wf(2)
        grouped[1] = regroup_block(1, *first_chunk)
        quantise_block(1, grouped[1], *first_chunk)
        grouped[5] = regroup_block(5, *first_chunk)
        quantise_wf(0)
        quantise_block(5, grouped[5], *first_chunk)
        grouped[2] = regroup_block(2, *first_chunk)
        quantise_wf(1)
        y_sums = {}

        def open_tiles(count, passes):
            for m in range(len(y_sums), count):
                y_sums[m] = sum_banks.tile([P, CHUNK], F32, name="y_sum")
                y_passes(y_sums[m], m, passes, *first_chunk, LAST)

        def block_passes(g):
            for m in y_sums:
                y_passes(y_sums[m], m, (g,), *first_chunk, LAST)

        open_tiles(2, (2,))
        transpose_wf(3)
        block_passes(0)
        quantise_block(2, grouped[2], *first_chunk)
        grouped[6] = regroup_block(6, *first_chunk)
        quantise_wf(2)
        open_tiles(3, (2, 0))
        block_passes(3)
        quantise_block(6, grouped[6], *first_chunk)
        quantise_wf(3)
        grouped[3] = regroup_block(3, *first_chunk)
        split_wf(4, nc.vector.tensor_copy)
        open_tiles(4, (2, 0, 3))
        block_passes(1)
        grouped[4] = regroup_block(4, *first_chunk, nc.scalar.copy)
        transpose_wf(4)
        quantise_block(3, grouped[3], *first_chunk)
        block_passes(4)
        split_wf(5, nc.vector.tensor_copy)
        transpose_wf(5)
        nc.vector.tensor_mul(out=gain[:], in0=gain[:], in1=per_channel["gf"][:])
        nc.vector.tensor_sub(out=shift[:], in0=per_channel["bfuse"][:], in1=per_channel["mf"][:])
        quantise_block(4, grouped[4], *first_chunk)
        nc.vector.tensor_mul(out=shift[:], in0=shift[:], in1=gain[:])
        quantise_wf(4)
        nc.vector.tensor_add(out=shift[:], in0=shift[:], in1=per_channel["bef"][:])
        split_wf(6, nc.vector.tensor_copy)
        for m in range(HALF):
            y_passes(y_sums[m], m, (LAST,), *first_chunk, LAST)
            finish_tile(y_sums[m], m, *first_chunk)
        prepare_next(0, FIRST_BLOCK_STEP)
        quantise_wf(5)
        split_wf(7, nc.vector.tensor_copy)

        for index, (col0, width) in enumerate(CHUNKS):
            for half in range(1 if index == 0 else 0, 2):
                tiles = range(half * HALF, (half + 1) * HALF)
                y_sums = {}
                for m in tiles:
                    prepare_next(index, 2 * half * HALF + m % HALF)
                    if index == 0 and m + WF_AHEAD < OUT_TILES:
                        transpose_wf(m + WF_AHEAD)
                    y_sums[m] = sum_banks.tile([P, CHUNK], F32, name="y_sum")
                    y_passes(y_sums[m], m, range(MID_PASSES, FUSED_PASSES), col0, width)
                    if index == 0 and m + WF_AHEAD < OUT_TILES:
                        quantise_wf(m + WF_AHEAD)
                for m in tiles:
                    prepare_next(index, (2 * half + 1) * HALF + m % HALF)
                    y_passes(y_sums[m], m, range(MID_PASSES), col0, width)
                    finish_tile(y_sums[m], m, col0, width)
